import numpy as np
import ml_dtypes


def mxq(x, axis, fmt="e4m3"):
    dtype, down = {"e4m3": (ml_dtypes.float8_e4m3fn, 7), "e5m2": (ml_dtypes.float8_e5m2, 14)}[fmt]
    v = np.moveaxis(np.asarray(x, np.float32).astype(ml_dtypes.bfloat16).astype(np.float64), axis, -1)
    blocks = v.reshape(v.shape[:-1] + (-1, 32))
    amax = np.abs(blocks).max(-1, keepdims=True)
    byte = np.maximum(np.where(amax > 0, np.frexp(amax)[1] - 1 + 127, 0) - down, 1)
    scale = np.exp2(byte - 127.0)
    codes = (blocks / scale).astype(np.float32).astype(dtype).astype(np.float64)
    return np.moveaxis((codes * scale).reshape(v.shape), -1, axis)


WIDE = False


def mx_kscale(k):
    if not WIDE:
        return np.ones(k)
    levels = np.array([10, -10, 5, -5, 0])
    if k % 512:
        return np.exp2(np.random.permutation(np.resize(levels, k // 32))).repeat(32)
    a = np.empty((k // 512, 16))
    for p in range(k // 512):
        a[p, :8] = np.random.permutation(np.resize(levels, 8))
        for g in range(8):
            far = levels[np.abs(levels - a[p, g]) >= 10]
            a[p, g + 8] = far[np.random.randint(len(far))]
    return np.exp2(a.ravel()).repeat(32)


BF16 = ml_dtypes.bfloat16


def bf(x):
    return np.asarray(x, np.float32).astype(BF16)


def f64(x):
    return np.asarray(x).astype(np.float64)


B, IN, H = 512, 1024, 1024


def sigmoid(v):
    return 1.0 / (1.0 + np.exp(-v))


def setup_inputs():
    s, t = mx_kscale(IN), mx_kscale(H)
    a = np.sqrt(2.0 / (IN + H))
    return {
        "x": bf(np.random.standard_normal((B, IN)) * s),
        "h_prev": bf(np.random.standard_normal((B, H)) * t),
        "m_prev": bf(np.random.standard_normal((B, H)) * 0.5),
        "Wi_x": bf(np.random.standard_normal((H, IN)) * a / s),
        "b_i": bf(np.random.standard_normal(H) * 0.3),
        "Wi_h": bf(np.random.standard_normal((H, H)) * a / t),
        "Wf_x": bf(np.random.standard_normal((H, IN)) * a / s),
        "b_f": bf(2.0 + np.random.standard_normal(H) * 0.3),
        "Wf_h": bf(np.random.standard_normal((H, H)) * a / t),
    }


def reference(x, h_prev, m_prev, Wi_x, b_i, Wi_h, Wf_x, b_f, Wf_h):
    xq = mxq(f64(x), 1, "e4m3")
    hq = mxq(f64(h_prev), 1, "e4m3")
    i_tilde = (xq @ mxq(f64(Wi_x), 1, "e4m3").T) + f64(b_i) + (hq @ mxq(f64(Wi_h), 1, "e4m3").T)
    f_aff = (xq @ mxq(f64(Wf_x), 1, "e4m3").T) + f64(b_f) + (hq @ mxq(f64(Wf_h), 1, "e4m3").T)
    log_f = np.log(np.maximum(sigmoid(f_aff), 1e-8))
    m_t = np.maximum(log_f + f64(m_prev), i_tilde)
    i_prime = np.exp(i_tilde - m_t)
    f_prime = np.exp(log_f + f64(m_prev) - m_t)
    return m_t, i_prime, f_prime

@@ -1,0 +1,261 @@
+from contextlib import ExitStack
+
+import concourse.mybir as mybir
+from concourse.masks import make_identity
+
+F32 = mybir.dt.float32
+BF16 = mybir.dt.bfloat16
+U32 = mybir.dt.uint32
+U8 = mybir.dt.uint8
+FP8X4 = mybir.dt.float8_e4m3fn_x4
+ACT = mybir.ActivationFunctionType
+ALU = mybir.AluOpType
+
+P = 128
+BATCH = 512
+SIDE_K = 1024
+HIDDEN = 1024
+K_PASS = 512
+SIDES = 2
+SIDE_PASSES = SIDE_K // K_PASS
+PASSES = SIDES * SIDE_PASSES
+BLOCK_ROWS = 256
+ROW_TILES = BLOCK_ROWS // P
+BATCH_TILES = BATCH // P
+CHUNKS = HIDDEN // BLOCK_ROWS
+SIDE_WORDS = SIDE_K // 2
+WORD_TILES = SIDE_WORDS // P
+SIGMOID_FLOOR = 1e-8
+
+FLOPS = 2 * BATCH * (SIDES * SIDE_K) * (2 * HIDDEN)
+
+
+def tile_slstmlayer_pa_kernel(
+    tc, x, h_prev, m_prev, Wi_x, b_i, Wi_h, Wf_x, b_f, Wf_h, out_0, out_1, out_2
+):
+    nc = tc.nc
+    with ExitStack() as ctx:
+        const = ctx.enter_context(tc.tile_pool(name="const", bufs=1))
+        raw_pool = ctx.enter_context(tc.tile_pool(name="raw", bufs=1))
+        grouped_pool = ctx.enter_context(tc.tile_pool(name="grouped", bufs=4))
+        act_pool = ctx.enter_context(tc.tile_pool(name="act_codes", bufs=1))
+        w_pool = ctx.enter_context(tc.tile_pool(name="w_codes", bufs=3))
+        keep = ctx.enter_context(tc.tile_pool(name="keep", bufs=1))
+        work = ctx.enter_context(tc.tile_pool(name="work", bufs=3))
+        t_psum = ctx.enter_context(tc.psum_pool(name="t_psum", bufs=4))
+        acc_psum = ctx.enter_context(tc.psum_pool(name="acc_psum", bufs=4))
+
+        ident = const.tile([P, P], F32, name="ident")
+        make_identity(nc, ident[:])
+
+        def by_batch(ap):
+            return ap.rearrange("(p t) n -> p t n", t=BATCH_TILES)
+
+        blocks = []
+        for pair in range(BATCH_TILES // ROW_TILES):
+            tiles = slice(pair * ROW_TILES, (pair + 1) * ROW_TILES)
+            blocks.append((by_batch(x)[:, tiles, :], by_batch(h_prev)[:, tiles, :]))
+        for w_x, w_h in ((Wf_x, Wf_h), (Wi_x, Wi_h)):
+            for c in range(CHUNKS):
+                rows = slice(c * BLOCK_ROWS, (c + 1) * BLOCK_ROWS)
+                blocks.append(
+                    (
+                        w_x[rows, :].rearrange("(t p) k -> p t k", p=P),
+                        w_h[rows, :].rearrange("(t p) k -> p t k", p=P),
+                    )
+                )
+        ACT_BLOCKS = BATCH_TILES // ROW_TILES
+        UNITS = 2 * CHUNKS
+
+        raw = []
+
+        def load_block(k):
+            sides = []
+            for s in range(SIDES):
+                t = raw_pool.tile([P, ROW_TILES * SIDE_K], BF16, name="raw_%d_%d" % (k, s))
+                nc.sync.dma_start(
+                    out=t[:].rearrange("p (t k) -> p t k", t=ROW_TILES), in_=blocks[k][s]
+                )
+                sides.append(t)
+            raw.append(sides)
+
+        bias_f = const.tile([P, HIDDEN], BF16, name="bias_f")
+        bias_i = const.tile([P, HIDDEN], BF16, name="bias_i")
+        m_raw = const.tile([P, BATCH_TILES, HIDDEN], BF16, name="m_raw")
+        for k in range(ACT_BLOCKS + 2):
+            load_block(k)
+        nc.sync.dma_start(out=bias_f[:], in_=b_f.partition_broadcast(P))
+        for k in range(ACT_BLOCKS + 2, ACT_BLOCKS + CHUNKS + 1):
+            load_block(k)
+        nc.sync.dma_start(out=m_raw[:], in_=by_batch(m_prev))
+        nc.sync.dma_start(out=bias_i[:], in_=b_i.partition_broadcast(P))
+        for k in range(ACT_BLOCKS + CHUNKS + 1, ACT_BLOCKS + UNITS):
+            load_block(k)
+
+        grouped = {}
+        codes = {}
+        scales = {}
+
+        def transpose_block(k):
+            for s in range(SIDES):
+                words = raw[k][s][:].bitcast(F32)
+                g = grouped_pool.tile(
+                    [P, SIDE_PASSES * BLOCK_ROWS * 4], BF16, name="grouped", align_bytes=64
+                )
+                g_words = g[:].bitcast(F32).rearrange(
+                    "p (g c u) -> p g c u", g=SIDE_PASSES, u=2
+                )
+                for t in range(ROW_TILES):
+                    bank = t_psum.tile([P, WORD_TILES, P], F32, name="bank")
+                    for j in range(WORD_TILES):
+                        g_pass, u = divmod(j, 2)
+                        first = t * SIDE_WORDS + g_pass * (K_PASS // 2)
+                        nc.tensor.transpose(
+                            bank[:, j, :], words[:, first + u : first + K_PASS // 2 : 2], ident[:]
+                        )
+                    nc.scalar.copy(
+                        out=g_words[:, :, t * P : (t + 1) * P, :],
+                        in_=bank[:].rearrange("p (g u) r -> p g r u", u=2),
+                    )
+                grouped[(k, s)] = g
+
+        def quantise_block(k):
+            pool = act_pool if k < ACT_BLOCKS else w_pool
+            tag = "act_%d" % k if k < ACT_BLOCKS else "w"
+            cd = pool.tile(
+                [P, PASSES * BLOCK_ROWS], U32, name="codes_" + tag, align_bytes=64
+            )
+            sc = pool.tile(
+                [P, PASSES * BLOCK_ROWS], U8, name="scales_" + tag, align_bytes=64
+            )
+            for s in range(SIDES):
+                cols = slice(s * SIDE_PASSES * BLOCK_ROWS, (s + 1) * SIDE_PASSES * BLOCK_ROWS)
+                nc.vector.quantize_mx(
+                    out=cd[:, cols].bitcast(FP8X4), scales=sc[:, cols], in_=grouped[(k, s)][:]
+                )
+            codes[k] = cd
+            scales[k] = sc
+
+        acc = {}
+
+        def multiply(u):
+            k = ACT_BLOCKS + u
+            for pair in range(ACT_BLOCKS):
+                bank = acc_psum.tile([P, ROW_TILES, BLOCK_ROWS], F32, name="acc")
+                for t in range(ROW_TILES):
+                    for q in range(PASSES):
+                        a_cols = slice(q * BLOCK_ROWS + t * P, q * BLOCK_ROWS + (t + 1) * P)
+                        w_cols = slice(q * BLOCK_ROWS, (q + 1) * BLOCK_ROWS)
+                        nc.tensor.matmul_mx(
+                            out=bank[:, t, :],
+                            lhsT=codes[pair][:, a_cols].bitcast(FP8X4),
+                            lhsT_scale=scales[pair][:, a_cols],
+                            rhs=codes[k][:, w_cols].bitcast(FP8X4),
+                            rhs_scale=scales[k][:, w_cols],
+                            start=(q == 0),
+                            stop=(q == PASSES - 1),
+                        )
+                acc[(u, pair)] = bank
+
+        pre = {}
+
+        def add_bias(u):
+            bias = bias_f if u < CHUNKS else bias_i
+            c = u % CHUNKS
+            feats = slice(c * BLOCK_ROWS, (c + 1) * BLOCK_ROWS)
+            out = work.tile([P, BATCH_TILES, BLOCK_ROWS], F32, name="pre")
+            for pair in range(ACT_BLOCKS):
+                nc.vector.tensor_tensor(
+                    out=out[:, pair * ROW_TILES : (pair + 1) * ROW_TILES, :],
+                    in0=acc[(u, pair)][:],
+                    in1=bias[:, feats].unsqueeze(1).to_broadcast([P, ROW_TILES, BLOCK_ROWS]),
+                    op=ALU.add,
+                )
+            pre[u] = out
+
+        decay = {}
+        halves = [slice(h * ROW_TILES, (h + 1) * ROW_TILES) for h in range(ACT_BLOCKS)]
+
+        def sigmoid(c):
+            t = keep.tile([P, BATCH_TILES, BLOCK_ROWS], F32, name="decay_%d" % c)
+            for h in halves:
+                nc.scalar.activation(out=t[:, h, :], in_=pre[c][:, h, :], func=ACT.Sigmoid)
+            decay[c] = t
+
+        def clamp(c):
+            t = decay[c]
+            for h in halves:
+                nc.vector.tensor_scalar_max(out=t[:, h, :], in0=t[:, h, :], scalar1=SIGMOID_FLOOR)
+
+        def log(c):
+            t = decay[c]
+            for h in halves:
+                nc.scalar.activation(out=t[:, h, :], in_=t[:, h, :], func=ACT.Ln)
+
+        def add_m_prev(c):
+            feats = slice(c * BLOCK_ROWS, (c + 1) * BLOCK_ROWS)
+            t = decay[c]
+            for h in halves:
+                nc.vector.tensor_tensor(
+                    out=t[:, h, :], in0=t[:, h, :], in1=m_raw[:, h, feats], op=ALU.add
+                )
+
+        exps = {}
+
+        def stabilise_stage(c):
+            feats = slice(c * BLOCK_ROWS, (c + 1) * BLOCK_ROWS)
+            i_tilde = pre[CHUNKS + c]
+            a = decay[c]
+            m_t = work.tile([P, BATCH_TILES, BLOCK_ROWS], F32, name="m_t")
+            i_p = work.tile([P, BATCH_TILES, BLOCK_ROWS], F32, name="i_p")
+            f_p = work.tile([P, BATCH_TILES, BLOCK_ROWS], F32, name="f_p")
+            for h in halves:
+                nc.vector.tensor_tensor(out=m_t[:, h, :], in0=a[:, h, :], in1=i_tilde[:, h, :], op=ALU.max)
+            for h in halves:
+                nc.sync.dma_start(out=by_batch(out_0)[:, h, feats], in_=m_t[:, h, :])
+            for h in halves:
+                nc.vector.tensor_tensor(
+                    out=i_tilde[:, h, :], in0=i_tilde[:, h, :], in1=a[:, h, :], op=ALU.subtract
+                )
+            for h in halves:
+                nc.vector.tensor_scalar_min(out=i_p[:, h, :], in0=i_tilde[:, h, :], scalar1=0.0)
+            for h in halves:
+                nc.vector.tensor_scalar(
+                    out=f_p[:, h, :], in0=i_tilde[:, h, :], scalar1=-1.0, scalar2=0.0,
+                    op0=ALU.mult, op1=ALU.min,
+                )
+            exps[c] = (i_p, f_p)
+
+        def exp_stage(c):
+            feats = slice(c * BLOCK_ROWS, (c + 1) * BLOCK_ROWS)
+            for t, out in zip(exps[c], (out_1, out_2)):
+                for h in halves:
+                    nc.scalar.activation(out=t[:, h, :], in_=t[:, h, :], func=ACT.Exp)
+                    nc.sync.dma_start(out=by_batch(out)[:, h, feats], in_=t[:, h, :])
+
+        ctx.enter_context(tc.manual_schedule())
+        for k in range(ACT_BLOCKS + 1):
+            transpose_block(k)
+            quantise_block(k)
+        for u in range(UNITS + 2):
+            logs = [2 * (u - CHUNKS - 1) + i for i in range(2)] if u in (CHUNKS + 1, CHUNKS + 2) else []
+            for c in logs:
+                log(c)
+            if u + 1 < UNITS:
+                transpose_block(ACT_BLOCKS + u + 1)
+            if u < UNITS:
+                multiply(u)
+            if 1 <= u <= UNITS:
+                add_bias(u - 1)
+            if 2 <= u <= CHUNKS + 1:
+                clamp(u - 2)
+            for c in logs:
+                add_m_prev(c)
+            if u + 1 < UNITS:
+                quantise_block(ACT_BLOCKS + u + 1)
+            if 1 <= u <= CHUNKS:
+                sigmoid(u - 1)
+            if CHUNKS + 1 <= u <= UNITS:
+                stabilise_stage(u - 1 - CHUNKS)
+            if CHUNKS + 2 <= u:
+                exp_stage(u - 2 - CHUNKS)

@@ -1,3 +1,4 @@
+import math
 from contextlib import ExitStack
 
 import concourse.mybir as mybir
@@ -22,10 +23,15 @@ PASSES = SIDES * SIDE_PASSES
 BLOCK_ROWS = 256
 ROW_TILES = BLOCK_ROWS // P
 BATCH_TILES = BATCH // P
+PAIRS = BATCH_TILES // ROW_TILES
+FEAT_TILES = HIDDEN // P
 CHUNKS = HIDDEN // BLOCK_ROWS
 SIDE_WORDS = SIDE_K // 2
-WORD_TILES = SIDE_WORDS // P
+PASS_WORDS = K_PASS // 2
 SIGMOID_FLOOR = 1e-8
+TINY = 1e-30
+RELU = (0, 1)
+FINE = (("act", 0),)
 
 FLOPS = 2 * BATCH * (SIDES * SIDE_K) * (2 * HIDDEN)
 
@@ -37,68 +43,91 @@ def tile_slstmlayer_pa_kernel(
     with ExitStack() as ctx:
         const = ctx.enter_context(tc.tile_pool(name="const", bufs=1))
         raw_pool = ctx.enter_context(tc.tile_pool(name="raw", bufs=1))
+        perm_pool = ctx.enter_context(tc.tile_pool(name="perm", bufs=4))
         grouped_pool = ctx.enter_context(tc.tile_pool(name="grouped", bufs=4))
         act_pool = ctx.enter_context(tc.tile_pool(name="act_codes", bufs=1))
         w_pool = ctx.enter_context(tc.tile_pool(name="w_codes", bufs=3))
         keep = ctx.enter_context(tc.tile_pool(name="keep", bufs=1))
-        work = ctx.enter_context(tc.tile_pool(name="work", bufs=3))
+        work = ctx.enter_context(tc.tile_pool(name="work", bufs=2))
         t_psum = ctx.enter_context(tc.psum_pool(name="t_psum", bufs=4))
         acc_psum = ctx.enter_context(tc.psum_pool(name="acc_psum", bufs=4))
 
         ident = const.tile([P, P], F32, name="ident")
         make_identity(nc, ident[:])
+        ident_bf = const.tile([P, P], BF16, name="ident_bf")
+        make_identity(nc, ident_bf[:])
+        warm = const.tile([P, 1], F32, name="warm")
+        nc.vector.memset(warm[:], 0.0)
+        nc.scalar.activation(out=warm[:], in_=warm[:], func=ACT.Sigmoid)
 
         def by_batch(ap):
             return ap.rearrange("(p t) n -> p t n", t=BATCH_TILES)
 
-        blocks = []
-        for pair in range(BATCH_TILES // ROW_TILES):
+        def act_block(pair):
             tiles = slice(pair * ROW_TILES, (pair + 1) * ROW_TILES)
-            blocks.append((by_batch(x)[:, tiles, :], by_batch(h_prev)[:, tiles, :]))
-        for w_x, w_h in ((Wf_x, Wf_h), (Wi_x, Wi_h)):
-            for c in range(CHUNKS):
-                rows = slice(c * BLOCK_ROWS, (c + 1) * BLOCK_ROWS)
-                blocks.append(
-                    (
-                        w_x[rows, :].rearrange("(t p) k -> p t k", p=P),
-                        w_h[rows, :].rearrange("(t p) k -> p t k", p=P),
-                    )
-                )
-        ACT_BLOCKS = BATCH_TILES // ROW_TILES
-        UNITS = 2 * CHUNKS
+            return by_batch(x)[:, tiles, :], by_batch(h_prev)[:, tiles, :]
 
-        raw = []
+        def weight_block(w_x, w_h, c):
+            rows = slice(c * BLOCK_ROWS, (c + 1) * BLOCK_ROWS)
+            return [w[rows, :].rearrange("(t p) k -> p t k", p=P) for w in (w_x, w_h)]
 
-        def load_block(k):
-            sides = []
+        source = {}
+        for pair in range(PAIRS):
+            source[("act", pair)] = act_block(pair)
+        for c in range(CHUNKS):
+            source[("f", c)] = weight_block(Wf_x, Wf_h, c)
+            source[("i", c)] = weight_block(Wi_x, Wi_h, c)
+
+        raw = {}
+
+        def load(b):
             for s in range(SIDES):
-                t = raw_pool.tile([P, ROW_TILES * SIDE_K], BF16, name="raw_%d_%d" % (k, s))
-                nc.sync.dma_start(
-                    out=t[:].rearrange("p (t k) -> p t k", t=ROW_TILES), in_=blocks[k][s]
-                )
-                sides.append(t)
-            raw.append(sides)
+                t = raw_pool.tile([P, ROW_TILES * SIDE_K], BF16, name="raw_%s_%d_%d" % (b[0], b[1], s))
+                view = t[:].rearrange("p (t k) -> p t k", t=ROW_TILES)
+                if b in FINE:
+                    for r in range(ROW_TILES):
+                        nc.sync.dma_start(out=view[:, r, :], in_=source[b][s][:, r, :])
+                else:
+                    nc.sync.dma_start(out=view, in_=source[b][s])
+                raw[(b, s)] = t
 
-        bias_f = const.tile([P, HIDDEN], BF16, name="bias_f")
+        bias_rows = const.tile([P, P], BF16, name="bias_rows")
+        nc.gpsimd.memset(bias_rows[:], 0.0)
+        bias_cols = const.tile([P, FEAT_TILES], F32, name="bias_cols")
         bias_i = const.tile([P, HIDDEN], BF16, name="bias_i")
         m_raw = const.tile([P, BATCH_TILES, HIDDEN], BF16, name="m_raw")
-        for k in range(ACT_BLOCKS + 2):
-            load_block(k)
-        nc.sync.dma_start(out=bias_f[:], in_=b_f.partition_broadcast(P))
-        for k in range(ACT_BLOCKS + 2, ACT_BLOCKS + CHUNKS + 1):
-            load_block(k)
+        F = [("f", c) for c in range(CHUNKS)]
+        I = [("i", c) for c in range(CHUNKS)]
+        A = [("act", pair) for pair in range(PAIRS)]
+        load(A[0])
+        nc.sync.dma_start(
+            out=bias_rows[0:FEAT_TILES, :], in_=b_f.rearrange("(c p) -> c p", p=P)
+        )
+        for b in (F[0], A[1], F[1]):
+            load(b)
+        for b in (F[2], F[3], I[0]):
+            load(b)
         nc.sync.dma_start(out=m_raw[:], in_=by_batch(m_prev))
         nc.sync.dma_start(out=bias_i[:], in_=b_i.partition_broadcast(P))
-        for k in range(ACT_BLOCKS + CHUNKS + 1, ACT_BLOCKS + UNITS):
-            load_block(k)
+        for b in I[1:]:
+            load(b)
 
+        words = {}
         grouped = {}
         codes = {}
         scales = {}
 
-        def transpose_block(k):
+        def permute(b):
             for s in range(SIDES):
-                words = raw[k][s][:].bitcast(F32)
+                t = perm_pool.tile([P, ROW_TILES * SIDE_WORDS], F32, name="perm")
+                nc.vector.tensor_copy(
+                    out=t[:].rearrange("p (r u k) -> p r u k", u=2, k=P),
+                    in_=raw[(b, s)][:].bitcast(F32).rearrange("p (r k u) -> p r u k", u=2, k=P),
+                )
+                words[(b, s)] = t
+
+        def transpose(b, vec=()):
+            for s in range(SIDES):
                 g = grouped_pool.tile(
                     [P, SIDE_PASSES * BLOCK_ROWS * 4], BF16, name="grouped", align_bytes=64
                 )
@@ -106,156 +135,244 @@ def tile_slstmlayer_pa_kernel(
                     "p (g c u) -> p g c u", g=SIDE_PASSES, u=2
                 )
                 for t in range(ROW_TILES):
-                    bank = t_psum.tile([P, WORD_TILES, P], F32, name="bank")
-                    for j in range(WORD_TILES):
+                    bank = t_psum.tile([P, SIDE_PASSES * 2, P], F32, name="bank")
+                    for j in range(SIDE_PASSES * 2):
                         g_pass, u = divmod(j, 2)
-                        first = t * SIDE_WORDS + g_pass * (K_PASS // 2)
-                        nc.tensor.transpose(
-                            bank[:, j, :], words[:, first + u : first + K_PASS // 2 : 2], ident[:]
-                        )
-                    nc.scalar.copy(
+                        first = t * SIDE_WORDS + g_pass * PASS_WORDS
+                        if (b, s) in words:
+                            src = words[(b, s)][:][:, first + u * P : first + (u + 1) * P]
+                        else:
+                            src = raw[(b, s)][:].bitcast(F32)[:, first + u : first + PASS_WORDS : 2]
+                        nc.tensor.transpose(bank[:, j, :], src, ident[:])
+                    copy = nc.vector.tensor_copy if (s, t) in vec else nc.scalar.copy
+                    copy(
                         out=g_words[:, :, t * P : (t + 1) * P, :],
                         in_=bank[:].rearrange("p (g u) r -> p g r u", u=2),
                     )
-                grouped[(k, s)] = g
+                grouped[(b, s)] = g
 
-        def quantise_block(k):
-            pool = act_pool if k < ACT_BLOCKS else w_pool
-            tag = "act_%d" % k if k < ACT_BLOCKS else "w"
-            cd = pool.tile(
-                [P, PASSES * BLOCK_ROWS], U32, name="codes_" + tag, align_bytes=64
+        def quantise_side(b, s, cd, sc):
+            cols = slice(s * SIDE_PASSES * BLOCK_ROWS, (s + 1) * SIDE_PASSES * BLOCK_ROWS)
+            nc.vector.quantize_mx(
+                out=cd[:, cols].bitcast(FP8X4), scales=sc[:, cols], in_=grouped[(b, s)][:]
             )
-            sc = pool.tile(
-                [P, PASSES * BLOCK_ROWS], U8, name="scales_" + tag, align_bytes=64
-            )
+
+        def quantise(b):
+            pool = act_pool if b[0] == "act" else w_pool
+            tag = "act_%d" % b[1] if b[0] == "act" else "w"
+            cd = pool.tile([P, PASSES * BLOCK_ROWS], U32, name="codes_" + tag, align_bytes=64)
+            sc = pool.tile([P, PASSES * BLOCK_ROWS], U8, name="scales_" + tag, align_bytes=64)
             for s in range(SIDES):
-                cols = slice(s * SIDE_PASSES * BLOCK_ROWS, (s + 1) * SIDE_PASSES * BLOCK_ROWS)
-                nc.vector.quantize_mx(
-                    out=cd[:, cols].bitcast(FP8X4), scales=sc[:, cols], in_=grouped[(k, s)][:]
-                )
-            codes[k] = cd
-            scales[k] = sc
+                quantise_side(b, s, cd, sc)
+            codes[b] = cd
+            scales[b] = sc
 
         acc = {}
 
-        def multiply(u):
-            k = ACT_BLOCKS + u
-            for pair in range(ACT_BLOCKS):
+        def multiply_f(c, pair):
+            b = F[c]
+            if pair == 0:
+                acc[b] = [
+                    acc_psum.tile([P, PAIRS, BLOCK_ROWS], F32, name="acc") for t in range(ROW_TILES)
+                ]
+            for t in range(ROW_TILES):
+                for q in range(PASSES):
+                    w_cols = slice(q * BLOCK_ROWS + t * P, q * BLOCK_ROWS + (t + 1) * P)
+                    a_cols = slice(q * BLOCK_ROWS, (q + 1) * BLOCK_ROWS)
+                    nc.tensor.matmul_mx(
+                        out=acc[b][t][:, pair, :],
+                        lhsT=codes[b][:, w_cols].bitcast(FP8X4),
+                        lhsT_scale=scales[b][:, w_cols],
+                        rhs=codes[A[pair]][:, a_cols].bitcast(FP8X4),
+                        rhs_scale=scales[A[pair]][:, a_cols],
+                        start=(q == 0),
+                        stop=(q == PASSES - 1),
+                    )
+
+        def multiply(b, pair):
+            bank = acc_psum.tile([P, ROW_TILES, BLOCK_ROWS], F32, name="acc")
+            for t in range(ROW_TILES):
+                for q in range(PASSES):
+                    a_cols = slice(q * BLOCK_ROWS + t * P, q * BLOCK_ROWS + (t + 1) * P)
+                    w_cols = slice(q * BLOCK_ROWS, (q + 1) * BLOCK_ROWS)
+                    nc.tensor.matmul_mx(
+                        out=bank[:, t, :],
+                        lhsT=codes[A[pair]][:, a_cols].bitcast(FP8X4),
+                        lhsT_scale=scales[A[pair]][:, a_cols],
+                        rhs=codes[b][:, w_cols].bitcast(FP8X4),
+                        rhs_scale=scales[b][:, w_cols],
+                        start=(q == 0),
+                        stop=(q == PASSES - 1),
+                    )
+            acc[(b, pair)] = bank
+
+        halves = [slice(h * ROW_TILES, (h + 1) * ROW_TILES) for h in range(PAIRS)]
+        shape = [P, BATCH_TILES, BLOCK_ROWS]
+
+        def feats(c):
+            return slice(c * BLOCK_ROWS, (c + 1) * BLOCK_ROWS)
+
+        def bias_of(bias, c):
+            return bias[:, feats(c)].unsqueeze(1).to_broadcast([P, ROW_TILES, BLOCK_ROWS])
+
+        logs = {}
+
+        def bias_columns():
+            bank = t_psum.tile([P, P], BF16, name="bank")
+            nc.tensor.transpose(bank[:], bias_rows[:], ident_bf[:])
+            nc.scalar.copy(out=bias_cols[:], in_=bank[:, 0:FEAT_TILES])
+
+        def sigmoid(c, t):
+            if t == 0:
+                logs[c] = keep.tile([P, ROW_TILES, PAIRS * BLOCK_ROWS], F32, name="logs_%d" % c)
+            j = c * ROW_TILES + t
+            nc.scalar.activation(
+                out=logs[c][:, t, :], in_=acc[F[c]][t][:].rearrange("p a b -> p (a b)"),
+                func=ACT.Sigmoid, bias=bias_cols[:, j : j + 1],
+            )
+
+        def log(c, t):
+            s = logs[c][:, t, :]
+            nc.scalar.activation(out=s, in_=s, func=ACT.Ln)
+
+        log_banks = {}
+        gate = {}
+        less = {}
+
+        def turn_log(c):
+            for pair in range(PAIRS):
                 bank = acc_psum.tile([P, ROW_TILES, BLOCK_ROWS], F32, name="acc")
-                for t in range(ROW_TILES):
-                    for q in range(PASSES):
-                        a_cols = slice(q * BLOCK_ROWS + t * P, q * BLOCK_ROWS + (t + 1) * P)
-                        w_cols = slice(q * BLOCK_ROWS, (q + 1) * BLOCK_ROWS)
-                        nc.tensor.matmul_mx(
-                            out=bank[:, t, :],
-                            lhsT=codes[pair][:, a_cols].bitcast(FP8X4),
-                            lhsT_scale=scales[pair][:, a_cols],
-                            rhs=codes[k][:, w_cols].bitcast(FP8X4),
-                            rhs_scale=scales[k][:, w_cols],
-                            start=(q == 0),
-                            stop=(q == PASSES - 1),
+                for r in range(ROW_TILES):
+                    for t in range(ROW_TILES):
+                        first = pair * BLOCK_ROWS + r * P
+                        nc.tensor.transpose(
+                            bank[:, r, t * P : (t + 1) * P], logs[c][:, t, first : first + P], ident[:]
                         )
-                acc[(u, pair)] = bank
+                log_banks[(c, pair)] = bank
 
-        pre = {}
-
-        def add_bias(u):
-            bias = bias_f if u < CHUNKS else bias_i
-            c = u % CHUNKS
-            feats = slice(c * BLOCK_ROWS, (c + 1) * BLOCK_ROWS)
-            out = work.tile([P, BATCH_TILES, BLOCK_ROWS], F32, name="pre")
-            for pair in range(ACT_BLOCKS):
-                nc.vector.tensor_tensor(
-                    out=out[:, pair * ROW_TILES : (pair + 1) * ROW_TILES, :],
-                    in0=acc[(u, pair)][:],
-                    in1=bias[:, feats].unsqueeze(1).to_broadcast([P, ROW_TILES, BLOCK_ROWS]),
-                    op=ALU.add,
+        def decay(c):
+            gate[c] = keep.tile(shape, F32, name="gate_%d" % c)
+            for pair, h in enumerate(halves):
+                nc.vector.scalar_tensor_tensor(
+                    out=gate[c][:, h, :], in0=log_banks[(c, pair)][:], scalar=math.log(SIGMOID_FLOOR),
+                    in1=m_raw[:, h, feats(c)], op0=ALU.max, op1=ALU.add,
                 )
-            pre[u] = out
-
-        decay = {}
-        halves = [slice(h * ROW_TILES, (h + 1) * ROW_TILES) for h in range(ACT_BLOCKS)]
-
-        def sigmoid(c):
-            t = keep.tile([P, BATCH_TILES, BLOCK_ROWS], F32, name="decay_%d" % c)
-            for h in halves:
-                nc.scalar.activation(out=t[:, h, :], in_=pre[c][:, h, :], func=ACT.Sigmoid)
-            decay[c] = t
-
-        def clamp(c):
-            t = decay[c]
-            for h in halves:
-                nc.vector.tensor_scalar_max(out=t[:, h, :], in0=t[:, h, :], scalar1=SIGMOID_FLOOR)
-
-        def log(c):
-            t = decay[c]
-            for h in halves:
-                nc.scalar.activation(out=t[:, h, :], in_=t[:, h, :], func=ACT.Ln)
-
-        def add_m_prev(c):
-            feats = slice(c * BLOCK_ROWS, (c + 1) * BLOCK_ROWS)
-            t = decay[c]
+            less[c] = keep.tile(shape, F32, name="less_%d" % c)
             for h in halves:
                 nc.vector.tensor_tensor(
-                    out=t[:, h, :], in0=t[:, h, :], in1=m_raw[:, h, feats], op=ALU.add
+                    out=less[c][:, h, :], in0=gate[c][:, h, :], in1=bias_of(bias_i, c), op=ALU.subtract
                 )
 
-        exps = {}
+        diff = {}
+        i_p = {}
+        f_p = {}
+        m_t = {}
 
-        def stabilise_stage(c):
-            feats = slice(c * BLOCK_ROWS, (c + 1) * BLOCK_ROWS)
-            i_tilde = pre[CHUNKS + c]
-            a = decay[c]
-            m_t = work.tile([P, BATCH_TILES, BLOCK_ROWS], F32, name="m_t")
-            i_p = work.tile([P, BATCH_TILES, BLOCK_ROWS], F32, name="i_p")
-            f_p = work.tile([P, BATCH_TILES, BLOCK_ROWS], F32, name="f_p")
-            for h in halves:
-                nc.vector.tensor_tensor(out=m_t[:, h, :], in0=a[:, h, :], in1=i_tilde[:, h, :], op=ALU.max)
-            for h in halves:
-                nc.sync.dma_start(out=by_batch(out_0)[:, h, feats], in_=m_t[:, h, :])
-            for h in halves:
-                nc.vector.tensor_tensor(
-                    out=i_tilde[:, h, :], in0=i_tilde[:, h, :], in1=a[:, h, :], op=ALU.subtract
-                )
-            for h in halves:
-                nc.vector.tensor_scalar_min(out=i_p[:, h, :], in0=i_tilde[:, h, :], scalar1=0.0)
-            for h in halves:
-                nc.vector.tensor_scalar(
-                    out=f_p[:, h, :], in0=i_tilde[:, h, :], scalar1=-1.0, scalar2=0.0,
-                    op0=ALU.mult, op1=ALU.min,
-                )
-            exps[c] = (i_p, f_p)
+        def new_tiles(c):
+            diff[c] = work.tile(shape, F32, name="diff")
+            i_p[c] = work.tile(shape, F32, name="i_p")
+            f_p[c] = work.tile(shape, F32, name="f_p")
+            m_t[c] = work.tile(shape, F32, name="m_t")
 
-        def exp_stage(c):
-            feats = slice(c * BLOCK_ROWS, (c + 1) * BLOCK_ROWS)
-            for t, out in zip(exps[c], (out_1, out_2)):
-                for h in halves:
-                    nc.scalar.activation(out=t[:, h, :], in_=t[:, h, :], func=ACT.Exp)
-                    nc.sync.dma_start(out=by_batch(out)[:, h, feats], in_=t[:, h, :])
+        def difference(c, pair):
+            h = halves[pair]
+            nc.vector.tensor_tensor(
+                out=diff[c][:, h, :], in0=acc[(I[c], pair)][:], in1=less[c][:, h, :], op=ALU.subtract
+            )
+
+        def split(c, pair):
+            h = halves[pair]
+            d = diff[c][:, h, :]
+            if pair in RELU:
+                nc.scalar.activation(out=f_p[c][:, h, :], in_=d, func=ACT.Relu)
+            else:
+                nc.vector.tensor_scalar_max(out=f_p[c][:, h, :], in0=d, scalar1=0.0)
+            nc.vector.tensor_scalar_min(out=i_p[c][:, h, :], in0=d, scalar1=0.0)
+
+        def stabiliser(c, pair):
+            h = halves[pair]
+            nc.vector.tensor_tensor(
+                out=m_t[c][:, h, :], in0=gate[c][:, h, :], in1=f_p[c][:, h, :], op=ALU.add
+            )
+            nc.sync.dma_start(out=by_batch(out_0)[:, h, feats(c)], in_=m_t[c][:, h, :])
+
+        e_f = {}
+
+        def exps(c, pair):
+            if pair == 0:
+                e_f[c] = work.tile(shape, F32, name="e_f")
+            h = halves[pair]
+            nc.scalar.activation(out=e_f[c][:, h, :], in_=f_p[c][:, h, :], func=ACT.Exp, scale=-1.0)
+            nc.sync.dma_start(out=by_batch(out_2)[:, h, feats(c)], in_=e_f[c][:, h, :])
+            nc.scalar.activation(out=i_p[c][:, h, :], in_=i_p[c][:, h, :], func=ACT.Exp)
+            nc.sync.dma_start(out=by_batch(out_1)[:, h, feats(c)], in_=i_p[c][:, h, :])
 
         ctx.enter_context(tc.manual_schedule())
-        for k in range(ACT_BLOCKS + 1):
-            transpose_block(k)
-            quantise_block(k)
-        for u in range(UNITS + 2):
-            logs = [2 * (u - CHUNKS - 1) + i for i in range(2)] if u in (CHUNKS + 1, CHUNKS + 2) else []
-            for c in logs:
-                log(c)
-            if u + 1 < UNITS:
-                transpose_block(ACT_BLOCKS + u + 1)
-            if u < UNITS:
-                multiply(u)
-            if 1 <= u <= UNITS:
-                add_bias(u - 1)
-            if 2 <= u <= CHUNKS + 1:
-                clamp(u - 2)
-            for c in logs:
-                add_m_prev(c)
-            if u + 1 < UNITS:
-                quantise_block(ACT_BLOCKS + u + 1)
-            if 1 <= u <= CHUNKS:
-                sigmoid(u - 1)
-            if CHUNKS + 1 <= u <= UNITS:
-                stabilise_stage(u - 1 - CHUNKS)
-            if CHUNKS + 2 <= u:
-                exp_stage(u - 2 - CHUNKS)
+        transpose(A[0], ((0,1),(1,1)))
+        bias_columns()
+        transpose(F[0], ((0,1),(1,1)))
+        quantise(A[0])
+        quantise(F[0])
+        transpose(A[1], ())
+        multiply_f(0, 0)
+        permute(F[1])
+        transpose(F[1], ())
+        quantise(A[1])
+        permute(F[2])
+        multiply_f(0, 1)
+        quantise(F[1])
+        transpose(F[2], ())
+        permute(F[3])
+        for pair in range(PAIRS):
+            multiply_f(1, pair)
+        for t in range(ROW_TILES):
+            sigmoid(0, t)
+        quantise(F[2])
+        transpose(F[3], ())
+        for pair in range(PAIRS):
+            multiply_f(2, pair)
+        for t in range(ROW_TILES):
+            sigmoid(1, t)
+        quantise(F[3])
+        for pair in range(PAIRS):
+            multiply_f(3, pair)
+        for t in range(ROW_TILES):
+            sigmoid(2, t)
+        for t in range(ROW_TILES):
+            sigmoid(3, t)
+        transpose(I[0], ((0,0),(0,1),(1,0),(1,1)))
+        for t in range(ROW_TILES):
+            log(0, t)
+        quantise(I[0])
+        for t in range(ROW_TILES):
+            log(1, t)
+        transpose(I[1], ())
+        turn_log(0)
+        for pair in range(PAIRS):
+            multiply(I[0], pair)
+        decay(0)
+        quantise(I[1])
+        for t in range(ROW_TILES):
+            log(2, t)
+        for t in range(ROW_TILES):
+            log(3, t)
+        for c in range(CHUNKS):
+            new_tiles(c)
+            if c + 2 < CHUNKS:
+                transpose(I[c + 2], ())
+            if c + 1 < CHUNKS:
+                turn_log(c + 1)
+            for pair in range(PAIRS):
+                difference(c, pair)
+            if c + 1 < CHUNKS:
+                for pair in range(PAIRS):
+                    multiply(I[c + 1], pair)
+            for pair in range(PAIRS):
+                split(c, pair)
+            if c + 1 < CHUNKS:
+                decay(c + 1)
+            if c + 2 < CHUNKS:
+                quantise(I[c + 2])
+            for pair in range(PAIRS):
+                exps(c, pair)
+                stabiliser(c, pair)

@@ -56,6 +56,8 @@ def tile_slstmlayer_pa_kernel(
         make_identity(nc, ident[:])
         ident_bf = const.tile([P, P], BF16, name="ident_bf")
         make_identity(nc, ident_bf[:])
+        tiny = const.tile([P, 1], F32, name="tiny")
+        nc.vector.memset(tiny[:], TINY)
         warm = const.tile([P, 1], F32, name="warm")
         nc.vector.memset(warm[:], 0.0)
         nc.scalar.activation(out=warm[:], in_=warm[:], func=ACT.Sigmoid)
@@ -233,7 +235,7 @@ def tile_slstmlayer_pa_kernel(
 
         def log(c, t):
             s = logs[c][:, t, :]
-            nc.scalar.activation(out=s, in_=s, func=ACT.Ln)
+            nc.scalar.activation(out=s, in_=s, func=ACT.Ln, bias=tiny[:])
 
         log_banks = {}
         gate = {}
@@ -309,7 +311,6 @@ def tile_slstmlayer_pa_kernel(
 
         ctx.enter_context(tc.manual_schedule())
         transpose(A[0], ((0,1),(1,1)))
-        bias_columns()
         transpose(F[0], ((0,1),(1,1)))
         quantise(A[0])
         quantise(F[0])
@@ -322,6 +323,7 @@ def tile_slstmlayer_pa_kernel(
         multiply_f(0, 1)
         quantise(F[1])
         transpose(F[2], ())
+        bias_columns()
         permute(F[3])
         for pair in range(PAIRS):
             multiply_f(1, pair)

@@ -30,7 +30,10 @@ SIDE_WORDS = SIDE_K // 2
 PASS_WORDS = K_PASS // 2
 SIGMOID_FLOOR = 1e-8
 TINY = 1e-30
-RELU = (0, 1)
+RELU = [(c, pair) for c in range(4) for pair in range(2)]
+LASTT = True
+GREL = []
+GADD = []
 FINE = (("act", 0),)
 
 FLOPS = 2 * BATCH * (SIDES * SIDE_K) * (2 * HIDDEN)
@@ -48,7 +51,7 @@ def tile_slstmlayer_pa_kernel(
         act_pool = ctx.enter_context(tc.tile_pool(name="act_codes", bufs=1))
         w_pool = ctx.enter_context(tc.tile_pool(name="w_codes", bufs=3))
         keep = ctx.enter_context(tc.tile_pool(name="keep", bufs=1))
-        work = ctx.enter_context(tc.tile_pool(name="work", bufs=2))
+        work = ctx.enter_context(tc.tile_pool(name="work", bufs=3))
         t_psum = ctx.enter_context(tc.psum_pool(name="t_psum", bufs=4))
         acc_psum = ctx.enter_context(tc.psum_pool(name="acc_psum", bufs=4))
 
@@ -119,55 +122,45 @@ def tile_slstmlayer_pa_kernel(
         codes = {}
         scales = {}
 
-        def permute(b):
-            for s in range(SIDES):
-                t = perm_pool.tile([P, ROW_TILES * SIDE_WORDS], F32, name="perm")
-                nc.vector.tensor_copy(
-                    out=t[:].rearrange("p (r u k) -> p r u k", u=2, k=P),
-                    in_=raw[(b, s)][:].bitcast(F32).rearrange("p (r k u) -> p r u k", u=2, k=P),
-                )
-                words[(b, s)] = t
+        def permute(b, s, copy):
+            t = perm_pool.tile([P, ROW_TILES * SIDE_WORDS], F32, name="perm")
+            copy(
+                out=t[:].rearrange("p (r u k) -> p r u k", u=2, k=P),
+                in_=raw[(b, s)][:].bitcast(F32).rearrange("p (r k u) -> p r u k", u=2, k=P),
+            )
+            words[(b, s)] = t
 
-        def transpose(b, vec=()):
-            for s in range(SIDES):
-                g = grouped_pool.tile(
-                    [P, SIDE_PASSES * BLOCK_ROWS * 4], BF16, name="grouped", align_bytes=64
+        def transpose(b, s, copies):
+            g = grouped_pool.tile(
+                [P, SIDE_PASSES * BLOCK_ROWS * 4], BF16, name="grouped", align_bytes=64
+            )
+            g_words = g[:].bitcast(F32).rearrange("p (g c u) -> p g c u", g=SIDE_PASSES, u=2)
+            for t in range(ROW_TILES):
+                bank = t_psum.tile([P, SIDE_PASSES * 2, P], F32, name="bank")
+                for j in range(SIDE_PASSES * 2):
+                    g_pass, u = divmod(j, 2)
+                    first = t * SIDE_WORDS + g_pass * PASS_WORDS
+                    if (b, s) in words:
+                        src = words[(b, s)][:][:, first + u * P : first + (u + 1) * P]
+                    else:
+                        src = raw[(b, s)][:].bitcast(F32)[:, first + u : first + PASS_WORDS : 2]
+                    nc.tensor.transpose(bank[:, j, :], src, ident[:])
+                copies[t](
+                    out=g_words[:, :, t * P : (t + 1) * P, :],
+                    in_=bank[:].rearrange("p (g u) r -> p g r u", u=2),
                 )
-                g_words = g[:].bitcast(F32).rearrange(
-                    "p (g c u) -> p g c u", g=SIDE_PASSES, u=2
-                )
-                for t in range(ROW_TILES):
-                    bank = t_psum.tile([P, SIDE_PASSES * 2, P], F32, name="bank")
-                    for j in range(SIDE_PASSES * 2):
-                        g_pass, u = divmod(j, 2)
-                        first = t * SIDE_WORDS + g_pass * PASS_WORDS
-                        if (b, s) in words:
-                            src = words[(b, s)][:][:, first + u * P : first + (u + 1) * P]
-                        else:
-                            src = raw[(b, s)][:].bitcast(F32)[:, first + u : first + PASS_WORDS : 2]
-                        nc.tensor.transpose(bank[:, j, :], src, ident[:])
-                    copy = nc.vector.tensor_copy if (s, t) in vec else nc.scalar.copy
-                    copy(
-                        out=g_words[:, :, t * P : (t + 1) * P, :],
-                        in_=bank[:].rearrange("p (g u) r -> p g r u", u=2),
-                    )
-                grouped[(b, s)] = g
+            grouped[(b, s)] = g
 
-        def quantise_side(b, s, cd, sc):
+        def quantise(b, s):
+            if s == 0:
+                pool = act_pool if b[0] == "act" else w_pool
+                tag = "act_%d" % b[1] if b[0] == "act" else "w"
+                codes[b] = pool.tile([P, PASSES * BLOCK_ROWS], U32, name="codes_" + tag, align_bytes=64)
+                scales[b] = pool.tile([P, PASSES * BLOCK_ROWS], U8, name="scales_" + tag, align_bytes=64)
             cols = slice(s * SIDE_PASSES * BLOCK_ROWS, (s + 1) * SIDE_PASSES * BLOCK_ROWS)
             nc.vector.quantize_mx(
-                out=cd[:, cols].bitcast(FP8X4), scales=sc[:, cols], in_=grouped[(b, s)][:]
+                out=codes[b][:, cols].bitcast(FP8X4), scales=scales[b][:, cols], in_=grouped[(b, s)][:]
             )
-
-        def quantise(b):
-            pool = act_pool if b[0] == "act" else w_pool
-            tag = "act_%d" % b[1] if b[0] == "act" else "w"
-            cd = pool.tile([P, PASSES * BLOCK_ROWS], U32, name="codes_" + tag, align_bytes=64)
-            sc = pool.tile([P, PASSES * BLOCK_ROWS], U8, name="scales_" + tag, align_bytes=64)
-            for s in range(SIDES):
-                quantise_side(b, s, cd, sc)
-            codes[b] = cd
-            scales[b] = sc
 
         acc = {}
 
@@ -192,7 +185,10 @@ def tile_slstmlayer_pa_kernel(
                     )
 
         def multiply(b, pair):
-            bank = acc_psum.tile([P, ROW_TILES, BLOCK_ROWS], F32, name="acc")
+            if b == I[-1] and LASTT:
+                bank = t_psum.tile([P, ROW_TILES, BLOCK_ROWS], F32, name="bank")
+            else:
+                bank = acc_psum.tile([P, ROW_TILES, BLOCK_ROWS], F32, name="acc")
             for t in range(ROW_TILES):
                 for q in range(PASSES):
                     a_cols = slice(q * BLOCK_ROWS + t * P, q * BLOCK_ROWS + (t + 1) * P)
@@ -259,122 +255,132 @@ def tile_slstmlayer_pa_kernel(
                     out=gate[c][:, h, :], in0=log_banks[(c, pair)][:], scalar=math.log(SIGMOID_FLOOR),
                     in1=m_raw[:, h, feats(c)], op0=ALU.max, op1=ALU.add,
                 )
-            less[c] = keep.tile(shape, F32, name="less_%d" % c)
+            less[c] = work.tile(shape, F32, name="less")
             for h in halves:
                 nc.vector.tensor_tensor(
                     out=less[c][:, h, :], in0=gate[c][:, h, :], in1=bias_of(bias_i, c), op=ALU.subtract
                 )
 
-        diff = {}
         i_p = {}
         f_p = {}
-        m_t = {}
-
-        def new_tiles(c):
-            diff[c] = work.tile(shape, F32, name="diff")
-            i_p[c] = work.tile(shape, F32, name="i_p")
-            f_p[c] = work.tile(shape, F32, name="f_p")
-            m_t[c] = work.tile(shape, F32, name="m_t")
+        rise = {}
 
         def difference(c, pair):
-            h = halves[pair]
-            nc.vector.tensor_tensor(
-                out=diff[c][:, h, :], in0=acc[(I[c], pair)][:], in1=less[c][:, h, :], op=ALU.subtract
-            )
+            d = less[c][:, halves[pair], :]
+            nc.vector.tensor_tensor(out=d, in0=acc[(I[c], pair)][:], in1=d, op=ALU.subtract)
 
         def split(c, pair):
+            if pair == 0:
+                i_p[c] = work.tile(shape, F32, name="i_p")
+                rise[c] = work.tile(shape, F32, name="rise")
             h = halves[pair]
-            d = diff[c][:, h, :]
-            if pair in RELU:
-                nc.scalar.activation(out=f_p[c][:, h, :], in_=d, func=ACT.Relu)
-            else:
-                nc.vector.tensor_scalar_max(out=f_p[c][:, h, :], in0=d, scalar1=0.0)
+            d = less[c][:, h, :]
+            r = rise[c][:, h, :]
             nc.vector.tensor_scalar_min(out=i_p[c][:, h, :], in0=d, scalar1=0.0)
+            if (c, pair) in GREL:
+                nc.gpsimd.tensor_scalar(
+                    out=r, in0=d, scalar1=0.0, scalar2=1.0, op0=ALU.max, op1=ALU.mult
+                )
+            elif (c, pair) in RELU:
+                nc.scalar.activation(out=r, in_=d, func=ACT.Relu)
+            else:
+                nc.vector.tensor_scalar_max(out=r, in0=d, scalar1=0.0)
 
         def stabiliser(c, pair):
             h = halves[pair]
-            nc.vector.tensor_tensor(
-                out=m_t[c][:, h, :], in0=gate[c][:, h, :], in1=f_p[c][:, h, :], op=ALU.add
-            )
-            nc.sync.dma_start(out=by_batch(out_0)[:, h, feats(c)], in_=m_t[c][:, h, :])
-
-        e_f = {}
+            m = gate[c][:, h, :]
+            eng = nc.gpsimd if (c, pair) in GADD else nc.vector
+            eng.tensor_tensor(out=m, in0=m, in1=rise[c][:, h, :], op=ALU.add)
+            nc.sync.dma_start(out=by_batch(out_0)[:, h, feats(c)], in_=m)
 
         def exps(c, pair):
             if pair == 0:
-                e_f[c] = work.tile(shape, F32, name="e_f")
+                f_p[c] = work.tile(shape, F32, name="f_p")
             h = halves[pair]
-            nc.scalar.activation(out=e_f[c][:, h, :], in_=f_p[c][:, h, :], func=ACT.Exp, scale=-1.0)
-            nc.sync.dma_start(out=by_batch(out_2)[:, h, feats(c)], in_=e_f[c][:, h, :])
-            nc.scalar.activation(out=i_p[c][:, h, :], in_=i_p[c][:, h, :], func=ACT.Exp)
-            nc.sync.dma_start(out=by_batch(out_1)[:, h, feats(c)], in_=i_p[c][:, h, :])
+            nc.scalar.activation(out=f_p[c][:, h, :], in_=rise[c][:, h, :], func=ACT.Exp, scale=-1.0)
+            nc.sync.dma_start(out=by_batch(out_2)[:, h, feats(c)], in_=f_p[c][:, h, :])
+            i_half = i_p[c][:, h, :]
+            nc.scalar.activation(out=i_half, in_=i_half, func=ACT.Exp)
+            nc.sync.dma_start(out=by_batch(out_1)[:, h, feats(c)], in_=i_half)
 
         ctx.enter_context(tc.manual_schedule())
-        transpose(A[0], ((0,1),(1,1)))
-        transpose(F[0], ((0,1),(1,1)))
-        quantise(A[0])
-        quantise(F[0])
-        transpose(A[1], ())
+        V = nc.vector.tensor_copy
+        S = nc.scalar.copy
+        SV = (S, V)
+        SS = (S, S)
+        VV = (V, V)
+
+        def each(fn, *args):
+            for i in range(2):
+                fn(*args, i)
+
+        transpose(A[0], 0, SV)
+        transpose(A[0], 1, SV)
+        quantise(A[0], 0)
+        transpose(F[0], 0, SV)
+        quantise(A[0], 1)
+        transpose(F[0], 1, SV)
+        quantise(F[0], 0)
+        transpose(A[1], 0, SS)
+        quantise(F[0], 1)
+        transpose(A[1], 1, SS)
         multiply_f(0, 0)
-        permute(F[1])
-        transpose(F[1], ())
-        quantise(A[1])
-        permute(F[2])
+        permute(F[1], 0, V)
+        permute(F[1], 1, V)
+        transpose(F[1], 0, SS)
+        quantise(A[1], 0)
+        transpose(F[1], 1, SS)
+        quantise(A[1], 1)
+        permute(F[2], 0, V)
+        permute(F[2], 1, V)
         multiply_f(0, 1)
-        quantise(F[1])
-        transpose(F[2], ())
-        bias_columns()
-        permute(F[3])
-        for pair in range(PAIRS):
-            multiply_f(1, pair)
-        for t in range(ROW_TILES):
-            sigmoid(0, t)
-        quantise(F[2])
-        transpose(F[3], ())
-        for pair in range(PAIRS):
-            multiply_f(2, pair)
-        for t in range(ROW_TILES):
-            sigmoid(1, t)
-        quantise(F[3])
-        for pair in range(PAIRS):
-            multiply_f(3, pair)
-        for t in range(ROW_TILES):
-            sigmoid(2, t)
-        for t in range(ROW_TILES):
-            sigmoid(3, t)
-        transpose(I[0], ((0,0),(0,1),(1,0),(1,1)))
-        for t in range(ROW_TILES):
-            log(0, t)
-        quantise(I[0])
-        for t in range(ROW_TILES):
-            log(1, t)
-        transpose(I[1], ())
-        turn_log(0)
-        for pair in range(PAIRS):
-            multiply(I[0], pair)
-        decay(0)
-        quantise(I[1])
-        for t in range(ROW_TILES):
-            log(2, t)
-        for t in range(ROW_TILES):
-            log(3, t)
-        for c in range(CHUNKS):
-            new_tiles(c)
+        quantise(F[1], 0)
+        quantise(F[1], 1)
+        for c in range(CHUNKS - 1):
             if c + 2 < CHUNKS:
-                transpose(I[c + 2], ())
+                transpose(F[c + 2], 0, SS)
+                transpose(F[c + 2], 1, SS)
+            if c == 0:
+                bias_columns()
+            if c + 3 < CHUNKS:
+                permute(F[c + 3], 0, V)
+                permute(F[c + 3], 1, V)
+            each(multiply_f, c + 1)
+            each(sigmoid, c)
+            if c + 2 < CHUNKS:
+                quantise(F[c + 2], 0)
+                quantise(F[c + 2], 1)
+        each(sigmoid, 3)
+        transpose(I[0], 0, VV)
+        transpose(I[0], 1, VV)
+        each(log, 0)
+        quantise(I[0], 0)
+        quantise(I[0], 1)
+        each(log, 1)
+        transpose(I[1], 0, SS)
+        transpose(I[1], 1, SS)
+        turn_log(0)
+        each(multiply, I[0])
+        decay(0)
+        quantise(I[1], 0)
+        quantise(I[1], 1)
+        each(log, 2)
+        each(log, 3)
+        for c in range(CHUNKS):
+            if c + 2 < CHUNKS:
+                transpose(I[c + 2], 0, SS)
+                transpose(I[c + 2], 1, SS)
             if c + 1 < CHUNKS:
                 turn_log(c + 1)
-            for pair in range(PAIRS):
-                difference(c, pair)
+            each(difference, c)
             if c + 1 < CHUNKS:
-                for pair in range(PAIRS):
-                    multiply(I[c + 1], pair)
-            for pair in range(PAIRS):
-                split(c, pair)
+                each(multiply, I[c + 1])
+            each(split, c)
             if c + 1 < CHUNKS:
                 decay(c + 1)
             if c + 2 < CHUNKS:
-                quantise(I[c + 2])
+                quantise(I[c + 2], 0)
+                quantise(I[c + 2], 1)
             for pair in range(PAIRS):
                 exps(c, pair)
                 stabiliser(c, pair)

import math
from contextlib import ExitStack

import concourse.mybir as mybir
from concourse.masks import make_identity

F32 = mybir.dt.float32
BF16 = mybir.dt.bfloat16
U32 = mybir.dt.uint32
U8 = mybir.dt.uint8
FP8X4 = mybir.dt.float8_e4m3fn_x4
ACT = mybir.ActivationFunctionType
ALU = mybir.AluOpType

P = 128
BATCH = 512
SIDE_K = 1024
HIDDEN = 1024
K_PASS = 512
SIDES = 2
SIDE_PASSES = SIDE_K // K_PASS
PASSES = SIDES * SIDE_PASSES
BLOCK_ROWS = 256
ROW_TILES = BLOCK_ROWS // P
BATCH_TILES = BATCH // P
PAIRS = BATCH_TILES // ROW_TILES
FEAT_TILES = HIDDEN // P
CHUNKS = HIDDEN // BLOCK_ROWS
SIDE_WORDS = SIDE_K // 2
PASS_WORDS = K_PASS // 2
SIGMOID_FLOOR = 1e-8
TINY = 1e-30
RELU = [(c, pair) for c in range(4) for pair in range(2)]
LASTT = True
GREL = []
GADD = []
FINE = (("act", 0),)

FLOPS = 2 * BATCH * (SIDES * SIDE_K) * (2 * HIDDEN)


def tile_slstmlayer_pa_kernel(
    tc, x, h_prev, m_prev, Wi_x, b_i, Wi_h, Wf_x, b_f, Wf_h, out_0, out_1, out_2
):
    nc = tc.nc
    with ExitStack() as ctx:
        const = ctx.enter_context(tc.tile_pool(name="const", bufs=1))
        raw_pool = ctx.enter_context(tc.tile_pool(name="raw", bufs=1))
        perm_pool = ctx.enter_context(tc.tile_pool(name="perm", bufs=4))
        grouped_pool = ctx.enter_context(tc.tile_pool(name="grouped", bufs=4))
        act_pool = ctx.enter_context(tc.tile_pool(name="act_codes", bufs=1))
        w_pool = ctx.enter_context(tc.tile_pool(name="w_codes", bufs=3))
        keep = ctx.enter_context(tc.tile_pool(name="keep", bufs=1))
        work = ctx.enter_context(tc.tile_pool(name="work", bufs=3))
        t_psum = ctx.enter_context(tc.psum_pool(name="t_psum", bufs=4))
        acc_psum = ctx.enter_context(tc.psum_pool(name="acc_psum", bufs=4))

        ident = const.tile([P, P], F32, name="ident")
        make_identity(nc, ident[:])
        ident_bf = const.tile([P, P], BF16, name="ident_bf")
        make_identity(nc, ident_bf[:])
        tiny = const.tile([P, 1], F32, name="tiny")
        nc.vector.memset(tiny[:], TINY)
        warm = const.tile([P, 1], F32, name="warm")
        nc.vector.memset(warm[:], 0.0)
        nc.scalar.activation(out=warm[:], in_=warm[:], func=ACT.Sigmoid)

        def by_batch(ap):
            return ap.rearrange("(p t) n -> p t n", t=BATCH_TILES)

        def act_block(pair):
            tiles = slice(pair * ROW_TILES, (pair + 1) * ROW_TILES)
            return by_batch(x)[:, tiles, :], by_batch(h_prev)[:, tiles, :]

        def weight_block(w_x, w_h, c):
            rows = slice(c * BLOCK_ROWS, (c + 1) * BLOCK_ROWS)
            return [w[rows, :].rearrange("(t p) k -> p t k", p=P) for w in (w_x, w_h)]

        source = {}
        for pair in range(PAIRS):
            source[("act", pair)] = act_block(pair)
        for c in range(CHUNKS):
            source[("f", c)] = weight_block(Wf_x, Wf_h, c)
            source[("i", c)] = weight_block(Wi_x, Wi_h, c)

        raw = {}

        def load(b):
            for s in range(SIDES):
                t = raw_pool.tile([P, ROW_TILES * SIDE_K], BF16, name="raw_%s_%d_%d" % (b[0], b[1], s))
                view = t[:].rearrange("p (t k) -> p t k", t=ROW_TILES)
                if b in FINE:
                    for r in range(ROW_TILES):
                        nc.sync.dma_start(out=view[:, r, :], in_=source[b][s][:, r, :])
                else:
                    nc.sync.dma_start(out=view, in_=source[b][s])
                raw[(b, s)] = t

        bias_rows = const.tile([P, P], BF16, name="bias_rows")
        nc.gpsimd.memset(bias_rows[:], 0.0)
        bias_cols = const.tile([P, FEAT_TILES], F32, name="bias_cols")
        bias_i = const.tile([P, HIDDEN], BF16, name="bias_i")
        m_raw = const.tile([P, BATCH_TILES, HIDDEN], BF16, name="m_raw")
        F = [("f", c) for c in range(CHUNKS)]
        I = [("i", c) for c in range(CHUNKS)]
        A = [("act", pair) for pair in range(PAIRS)]
        load(A[0])
        nc.sync.dma_start(
            out=bias_rows[0:FEAT_TILES, :], in_=b_f.rearrange("(c p) -> c p", p=P)
        )
        for b in (F[0], A[1], F[1]):
            load(b)
        for b in (F[2], F[3], I[0]):
            load(b)
        nc.sync.dma_start(out=m_raw[:], in_=by_batch(m_prev))
        nc.sync.dma_start(out=bias_i[:], in_=b_i.partition_broadcast(P))
        for b in I[1:]:
            load(b)

        words = {}
        grouped = {}
        codes = {}
        scales = {}

        def permute(b, s, copy):
            t = perm_pool.tile([P, ROW_TILES * SIDE_WORDS], F32, name="perm")
            copy(
                out=t[:].rearrange("p (r u k) -> p r u k", u=2, k=P),
                in_=raw[(b, s)][:].bitcast(F32).rearrange("p (r k u) -> p r u k", u=2, k=P),
            )
            words[(b, s)] = t

        def transpose(b, s, copies):
            g = grouped_pool.tile(
                [P, SIDE_PASSES * BLOCK_ROWS * 4], BF16, name="grouped", align_bytes=64
            )
            g_words = g[:].bitcast(F32).rearrange("p (g c u) -> p g c u", g=SIDE_PASSES, u=2)
            for t in range(ROW_TILES):
                bank = t_psum.tile([P, SIDE_PASSES * 2, P], F32, name="bank")
                for j in range(SIDE_PASSES * 2):
                    g_pass, u = divmod(j, 2)
                    first = t * SIDE_WORDS + g_pass * PASS_WORDS
                    if (b, s) in words:
                        src = words[(b, s)][:][:, first + u * P : first + (u + 1) * P]
                    else:
                        src = raw[(b, s)][:].bitcast(F32)[:, first + u : first + PASS_WORDS : 2]
                    nc.tensor.transpose(bank[:, j, :], src, ident[:])
                copies[t](
                    out=g_words[:, :, t * P : (t + 1) * P, :],
                    in_=bank[:].rearrange("p (g u) r -> p g r u", u=2),
                )
            grouped[(b, s)] = g

        def quantise(b, s):
            if s == 0:
                pool = act_pool if b[0] == "act" else w_pool
                tag = "act_%d" % b[1] if b[0] == "act" else "w"
                codes[b] = pool.tile([P, PASSES * BLOCK_ROWS], U32, name="codes_" + tag, align_bytes=64)
                scales[b] = pool.tile([P, PASSES * BLOCK_ROWS], U8, name="scales_" + tag, align_bytes=64)
            cols = slice(s * SIDE_PASSES * BLOCK_ROWS, (s + 1) * SIDE_PASSES * BLOCK_ROWS)
            nc.vector.quantize_mx(
                out=codes[b][:, cols].bitcast(FP8X4), scales=scales[b][:, cols], in_=grouped[(b, s)][:]
            )

        acc = {}

        def multiply_f(c, pair):
            b = F[c]
            if pair == 0:
                acc[b] = [
                    acc_psum.tile([P, PAIRS, BLOCK_ROWS], F32, name="acc") for t in range(ROW_TILES)
                ]
            for t in range(ROW_TILES):
                for q in range(PASSES):
                    w_cols = slice(q * BLOCK_ROWS + t * P, q * BLOCK_ROWS + (t + 1) * P)
                    a_cols = slice(q * BLOCK_ROWS, (q + 1) * BLOCK_ROWS)
                    nc.tensor.matmul_mx(
                        out=acc[b][t][:, pair, :],
                        lhsT=codes[b][:, w_cols].bitcast(FP8X4),
                        lhsT_scale=scales[b][:, w_cols],
                        rhs=codes[A[pair]][:, a_cols].bitcast(FP8X4),
                        rhs_scale=scales[A[pair]][:, a_cols],
                        start=(q == 0),
                        stop=(q == PASSES - 1),
                    )

        def multiply(b, pair):
            if b == I[-1] and LASTT:
                bank = t_psum.tile([P, ROW_TILES, BLOCK_ROWS], F32, name="bank")
            else:
                bank = acc_psum.tile([P, ROW_TILES, BLOCK_ROWS], F32, name="acc")
            for t in range(ROW_TILES):
                for q in range(PASSES):
                    a_cols = slice(q * BLOCK_ROWS + t * P, q * BLOCK_ROWS + (t + 1) * P)
                    w_cols = slice(q * BLOCK_ROWS, (q + 1) * BLOCK_ROWS)
                    nc.tensor.matmul_mx(
                        out=bank[:, t, :],
                        lhsT=codes[A[pair]][:, a_cols].bitcast(FP8X4),
                        lhsT_scale=scales[A[pair]][:, a_cols],
                        rhs=codes[b][:, w_cols].bitcast(FP8X4),
                        rhs_scale=scales[b][:, w_cols],
                        start=(q == 0),
                        stop=(q == PASSES - 1),
                    )
            acc[(b, pair)] = bank

        halves = [slice(h * ROW_TILES, (h + 1) * ROW_TILES) for h in range(PAIRS)]
        shape = [P, BATCH_TILES, BLOCK_ROWS]

        def feats(c):
            return slice(c * BLOCK_ROWS, (c + 1) * BLOCK_ROWS)

        def bias_of(bias, c):
            return bias[:, feats(c)].unsqueeze(1).to_broadcast([P, ROW_TILES, BLOCK_ROWS])

        logs = {}

        def bias_columns():
            bank = t_psum.tile([P, P], BF16, name="bank")
            nc.tensor.transpose(bank[:], bias_rows[:], ident_bf[:])
            nc.scalar.copy(out=bias_cols[:], in_=bank[:, 0:FEAT_TILES])

        def sigmoid(c, t):
            if t == 0:
                logs[c] = keep.tile([P, ROW_TILES, PAIRS * BLOCK_ROWS], F32, name="logs_%d" % c)
            j = c * ROW_TILES + t
            nc.scalar.activation(
                out=logs[c][:, t, :], in_=acc[F[c]][t][:].rearrange("p a b -> p (a b)"),
                func=ACT.Sigmoid, bias=bias_cols[:, j : j + 1],
            )

        def log(c, t):
            s = logs[c][:, t, :]
            nc.scalar.activation(out=s, in_=s, func=ACT.Ln, bias=tiny[:])

        log_banks = {}
        gate = {}
        less = {}

        def turn_log(c):
            for pair in range(PAIRS):
                bank = acc_psum.tile([P, ROW_TILES, BLOCK_ROWS], F32, name="acc")
                for r in range(ROW_TILES):
                    for t in range(ROW_TILES):
                        first = pair * BLOCK_ROWS + r * P
                        nc.tensor.transpose(
                            bank[:, r, t * P : (t + 1) * P], logs[c][:, t, first : first + P], ident[:]
                        )
                log_banks[(c, pair)] = bank

        def decay(c):
            gate[c] = keep.tile(shape, F32, name="gate_%d" % c)
            for pair, h in enumerate(halves):
                nc.vector.scalar_tensor_tensor(
                    out=gate[c][:, h, :], in0=log_banks[(c, pair)][:], scalar=math.log(SIGMOID_FLOOR),
                    in1=m_raw[:, h, feats(c)], op0=ALU.max, op1=ALU.add,
                )
            less[c] = work.tile(shape, F32, name="less")
            for h in halves:
                nc.vector.tensor_tensor(
                    out=less[c][:, h, :], in0=gate[c][:, h, :], in1=bias_of(bias_i, c), op=ALU.subtract
                )

        i_p = {}
        f_p = {}
        rise = {}

        def difference(c, pair):
            d = less[c][:, halves[pair], :]
            nc.vector.tensor_tensor(out=d, in0=acc[(I[c], pair)][:], in1=d, op=ALU.subtract)

        def split(c, pair):
            if pair == 0:
                i_p[c] = work.tile(shape, F32, name="i_p")
                rise[c] = work.tile(shape, F32, name="rise")
            h = halves[pair]
            d = less[c][:, h, :]
            r = rise[c][:, h, :]
            nc.vector.tensor_scalar_min(out=i_p[c][:, h, :], in0=d, scalar1=0.0)
            if (c, pair) in GREL:
                nc.gpsimd.tensor_scalar(
                    out=r, in0=d, scalar1=0.0, scalar2=1.0, op0=ALU.max, op1=ALU.mult
                )
            elif (c, pair) in RELU:
                nc.scalar.activation(out=r, in_=d, func=ACT.Relu)
            else:
                nc.vector.tensor_scalar_max(out=r, in0=d, scalar1=0.0)

        def stabiliser(c, pair):
            h = halves[pair]
            m = gate[c][:, h, :]
            eng = nc.gpsimd if (c, pair) in GADD else nc.vector
            eng.tensor_tensor(out=m, in0=m, in1=rise[c][:, h, :], op=ALU.add)
            nc.sync.dma_start(out=by_batch(out_0)[:, h, feats(c)], in_=m)

        def exps(c, pair):
            if pair == 0:
                f_p[c] = work.tile(shape, F32, name="f_p")
            h = halves[pair]
            nc.scalar.activation(out=f_p[c][:, h, :], in_=rise[c][:, h, :], func=ACT.Exp, scale=-1.0)
            nc.sync.dma_start(out=by_batch(out_2)[:, h, feats(c)], in_=f_p[c][:, h, :])
            i_half = i_p[c][:, h, :]
            nc.scalar.activation(out=i_half, in_=i_half, func=ACT.Exp)
            nc.sync.dma_start(out=by_batch(out_1)[:, h, feats(c)], in_=i_half)

        ctx.enter_context(tc.manual_schedule())
        V = nc.vector.tensor_copy
        S = nc.scalar.copy
        SV = (S, V)
        SS = (S, S)
        VV = (V, V)

        def each(fn, *args):
            for i in range(2):
                fn(*args, i)

        transpose(A[0], 0, SV)
        transpose(A[0], 1, SV)
        quantise(A[0], 0)
        transpose(F[0], 0, SV)
        quantise(A[0], 1)
        transpose(F[0], 1, SV)
        quantise(F[0], 0)
        transpose(A[1], 0, SS)
        quantise(F[0], 1)
        transpose(A[1], 1, SS)
        multiply_f(0, 0)
        permute(F[1], 0, V)
        permute(F[1], 1, V)
        transpose(F[1], 0, SS)
        quantise(A[1], 0)
        transpose(F[1], 1, SS)
        quantise(A[1], 1)
        permute(F[2], 0, V)
        permute(F[2], 1, V)
        multiply_f(0, 1)
        quantise(F[1], 0)
        quantise(F[1], 1)
        for c in range(CHUNKS - 1):
            if c + 2 < CHUNKS:
                transpose(F[c + 2], 0, SS)
                transpose(F[c + 2], 1, SS)
            if c == 0:
                bias_columns()
            if c + 3 < CHUNKS:
                permute(F[c + 3], 0, V)
                permute(F[c + 3], 1, V)
            each(multiply_f, c + 1)
            each(sigmoid, c)
            if c + 2 < CHUNKS:
                quantise(F[c + 2], 0)
                quantise(F[c + 2], 1)
        each(sigmoid, 3)
        transpose(I[0], 0, VV)
        transpose(I[0], 1, VV)
        each(log, 0)
        quantise(I[0], 0)
        quantise(I[0], 1)
        each(log, 1)
        transpose(I[1], 0, SS)
        transpose(I[1], 1, SS)
        turn_log(0)
        each(multiply, I[0])
        decay(0)
        quantise(I[1], 0)
        quantise(I[1], 1)
        each(log, 2)
        each(log, 3)
        for c in range(CHUNKS):
            if c + 2 < CHUNKS:
                transpose(I[c + 2], 0, SS)
                transpose(I[c + 2], 1, SS)
            if c + 1 < CHUNKS:
                turn_log(c + 1)
            each(difference, c)
            if c + 1 < CHUNKS:
                each(multiply, I[c + 1])
            each(split, c)
            if c + 1 < CHUNKS:
                decay(c + 1)
            if c + 2 < CHUNKS:
                quantise(I[c + 2], 0)
                quantise(I[c + 2], 1)
            for pair in range(PAIRS):
                exps(c, pair)
                stabiliser(c, pair)
